import numpy as np
import ml_dtypes

BF16 = ml_dtypes.bfloat16


def bf(x):
    return np.asarray(x, np.float32).astype(BF16)


def f32(x):
    return np.asarray(x, np.float32)


def f64(x):
    return np.asarray(x).astype(np.float64)


def striped(idx):
    return np.tile(idx.reshape(-1, 16).T, (8, 1))


D, S, M, N = 128, 512, 256, 512


def setup_inputs():
    return {
        "table": bf(np.random.standard_normal((D, S))),
        "w": bf(np.random.standard_normal((D, M)) / np.sqrt(D + D)),
        "recv": bf(np.random.standard_normal((D, N))),
        "w_recv": bf(np.random.standard_normal((D, M)) / np.sqrt(D + D)),
        "b1": f32(0.1 * np.random.standard_normal((M, 1))),
        "w3": bf(np.random.standard_normal((M, D)) / np.sqrt(M)),
        "b3": f32(0.1 * np.random.standard_normal((D, 1))),
        "offs": striped(np.random.permutation(S)[:N]),
    }


def reference(table, w, recv, w_recv, b1, w3, b3, offs):
    idx = offs[:16].T.reshape(-1)
    h = np.maximum(f64(w).T @ f64(table)[:, idx] + f64(w_recv).T @ f64(recv) + f64(b1), 0.0)
    return np.maximum(f64(w3).T @ h + f64(b3), 0.0) + f64(recv)

@@ -1,0 +1,60 @@
+import concourse.mybir as mybir
+
+BF16, F32, U16 = mybir.dt.bfloat16, mybir.dt.float32, mybir.dt.uint16
+RELU = mybir.ActivationFunctionType.Relu
+ADD, MAX = mybir.AluOpType.add, mybir.AluOpType.max
+
+P = 128
+S = 512
+N = 512
+M = 256
+HALVES = M // P
+
+FLOPS = 2 * N * (P * M + P * M + M * P)
+
+
+def tile_physics_kernel(tc, table, w, recv, w_recv, b1, w3, b3, offs, out):
+    nc = tc.nc
+    with tc.tile_pool(name="held", bufs=1) as held, tc.psum_pool(name="psum", bufs=1) as psum:
+        offsets = held.tile([P, N // 16], U16, name="offsets")
+        nc.sync.dma_start(offsets[:], offs)
+        table_sb = held.tile([P, S], BF16, name="table_sb")
+        nc.sync.dma_start(table_sb[:], table)
+        w_sb = held.tile([P, M], BF16, name="w_sb")
+        nc.scalar.dma_start(w_sb[:], w)
+        w_recv_sb = held.tile([P, M], BF16, name="w_recv_sb")
+        nc.scalar.dma_start(w_recv_sb[:], w_recv)
+        recv_sb = held.tile([P, N], BF16, name="recv_sb")
+        nc.sync.dma_start(recv_sb[:], recv)
+        b1_sb = []
+        w3_sb = []
+        for half in range(HALVES):
+            rows = slice(half * P, (half + 1) * P)
+            b1_sb.append(held.tile([P, 1], F32, name=f"b1_sb{half}"))
+            nc.scalar.dma_start(b1_sb[half][:], b1[rows, :])
+            w3_sb.append(held.tile([P, P], BF16, name=f"w3_sb{half}"))
+            nc.sync.dma_start(w3_sb[half][:], w3[rows, :])
+        b3_sb = held.tile([P, 1], F32, name="b3_sb")
+        nc.scalar.dma_start(b3_sb[:], b3)
+
+        hidden = []
+        for half in range(HALVES):
+            cols = slice(half * P, (half + 1) * P)
+            pre = psum.tile([P, N], F32, name=f"pre{half}")
+            nc.tensor.matmul(pre[:], w_sb[:, cols], table_sb[:].indirect(offsets[:]), start=True, stop=False)
+            nc.tensor.matmul(pre[:], w_recv_sb[:, cols], recv_sb[:], start=False, stop=True)
+            hidden.append(held.tile([P, N], BF16, name=f"hidden{half}"))
+            if half == 0:
+                nc.scalar.activation(hidden[half][:], pre[:], RELU, bias=b1_sb[half][:])
+            else:
+                nc.vector.tensor_scalar(hidden[half][:], pre[:], b1_sb[half][:], 0.0, ADD, MAX)
+
+        effect = psum.tile([P, N], F32, name="effect")
+        for half in range(HALVES):
+            nc.tensor.matmul(effect[:], w3_sb[half][:], hidden[half][:], start=half == 0, stop=half == HALVES - 1)
+
+        rectified = held.tile([P, N], F32, name="rectified")
+        nc.scalar.activation(rectified[:], effect[:], RELU, bias=b3_sb[:])
+        result = held.tile([P, N], F32, name="result")
+        nc.vector.tensor_tensor(result[:], rectified[:], recv_sb[:], ADD)
+        nc.sync.dma_start(out, result[:])

@@ -10,6 +10,8 @@ N = 512
 M = 256
 HALVES = M // P
 
+WARM_UP_MATMULS = 5
+
 FLOPS = 2 * N * (P * M + P * M + M * P)
 
 
@@ -36,6 +38,14 @@ def tile_physics_kernel(tc, table, w, recv, w_recv, b1, w3, b3, offs, out):
             nc.sync.dma_start(w3_sb[half][:], w3[rows, :])
         b3_sb = held.tile([P, 1], F32, name="b3_sb")
         nc.scalar.dma_start(b3_sb[:], b3)
+
+        zeros = held.tile([P, N], BF16, name="zeros")
+        nc.gpsimd.memset(zeros[:], 0.0)
+        unread = psum.tile([P, N], F32, name="unread")
+        for repeat in range(WARM_UP_MATMULS):
+            nc.tensor.matmul(unread[:], zeros[:, 0:P], zeros[:], start=True, stop=True)
+        unread_relu = held.tile([P, 1], BF16, name="unread_relu")
+        nc.scalar.activation(unread_relu[:], zeros[:, 0:1], RELU)
 
         hidden = []
         for half in range(HALVES):

@@ -9,8 +9,9 @@ S = 512
 N = 512
 M = 256
 HALVES = M // P
-
-WARM_UP_MATMULS = 5
+CHUNK = 256
+CHUNKS = N // CHUNK
+WARM_UP_MATMULS = 4
 
 FLOPS = 2 * N * (P * M + P * M + M * P)
 
@@ -33,38 +34,42 @@ def tile_physics_kernel(tc, table, w, recv, w_recv, b1, w3, b3, offs, out):
         for half in range(HALVES):
             rows = slice(half * P, (half + 1) * P)
             b1_sb.append(held.tile([P, 1], F32, name=f"b1_sb{half}"))
-            nc.scalar.dma_start(b1_sb[half][:], b1[rows, :])
+            nc.gpsimd.dma_start(b1_sb[half][:], b1[rows, :])
             w3_sb.append(held.tile([P, P], BF16, name=f"w3_sb{half}"))
             nc.sync.dma_start(w3_sb[half][:], w3[rows, :])
         b3_sb = held.tile([P, 1], F32, name="b3_sb")
-        nc.scalar.dma_start(b3_sb[:], b3)
+        nc.gpsimd.dma_start(b3_sb[:], b3)
 
-        zeros = held.tile([P, N], BF16, name="zeros")
-        nc.gpsimd.memset(zeros[:], 0.0)
-        unread = psum.tile([P, N], F32, name="unread")
+        zeros = held.tile([P, P], BF16, name="zeros")
+        nc.vector.memset(zeros[:], 0.0)
+        unread = psum.tile([P, N // P, P], F32, name="unread")
         for repeat in range(WARM_UP_MATMULS):
-            nc.tensor.matmul(unread[:], zeros[:, 0:P], zeros[:], start=True, stop=True)
+            nc.tensor.matmul(unread[:], zeros[:], zeros[:].unsqueeze(1).to_broadcast([P, N // P, P]), start=True, stop=True)
         unread_relu = held.tile([P, 1], BF16, name="unread_relu")
         nc.scalar.activation(unread_relu[:], zeros[:, 0:1], RELU)
 
-        hidden = []
-        for half in range(HALVES):
-            cols = slice(half * P, (half + 1) * P)
-            pre = psum.tile([P, N], F32, name=f"pre{half}")
-            nc.tensor.matmul(pre[:], w_sb[:, cols], table_sb[:].indirect(offsets[:]), start=True, stop=False)
-            nc.tensor.matmul(pre[:], w_recv_sb[:, cols], recv_sb[:], start=False, stop=True)
-            hidden.append(held.tile([P, N], BF16, name=f"hidden{half}"))
-            if half == 0:
-                nc.scalar.activation(hidden[half][:], pre[:], RELU, bias=b1_sb[half][:])
-            else:
-                nc.vector.tensor_scalar(hidden[half][:], pre[:], b1_sb[half][:], 0.0, ADD, MAX)
+        hidden = {}
+        for chunk in range(CHUNKS):
+            cols = slice(chunk * CHUNK, (chunk + 1) * CHUNK)
+            senders = table_sb[:].indirect(offsets[:, chunk * CHUNK // 16 : (chunk + 1) * CHUNK // 16])
+            for half in range(HALVES):
+                units = slice(half * P, (half + 1) * P)
+                pre = psum.tile([P, CHUNK], F32, name=f"pre{chunk}_{half}")
+                nc.tensor.matmul(pre[:], w_sb[:, units], senders, start=True, stop=False)
+                nc.tensor.matmul(pre[:], w_recv_sb[:, units], recv_sb[:, cols], start=False, stop=True)
+                hidden[chunk, half] = held.tile([P, CHUNK], BF16, name=f"hidden{chunk}_{half}")
+                if half == 0:
+                    nc.scalar.activation(hidden[chunk, half][:], pre[:], RELU, bias=b1_sb[half][:])
+                else:
+                    nc.vector.tensor_scalar(hidden[chunk, half][:], pre[:], b1_sb[half][:], 0.0, ADD, MAX)
 
-        effect = psum.tile([P, N], F32, name="effect")
-        for half in range(HALVES):
-            nc.tensor.matmul(effect[:], w3_sb[half][:], hidden[half][:], start=half == 0, stop=half == HALVES - 1)
-
-        rectified = held.tile([P, N], F32, name="rectified")
-        nc.scalar.activation(rectified[:], effect[:], RELU, bias=b3_sb[:])
-        result = held.tile([P, N], F32, name="result")
-        nc.vector.tensor_tensor(result[:], rectified[:], recv_sb[:], ADD)
-        nc.sync.dma_start(out, result[:])
+        for chunk in range(CHUNKS):
+            cols = slice(chunk * CHUNK, (chunk + 1) * CHUNK)
+            effect = psum.tile([P, CHUNK], F32, name=f"effect{chunk}")
+            for half in range(HALVES):
+                nc.tensor.matmul(effect[:], w3_sb[half][:], hidden[chunk, half][:], start=half == 0, stop=half == HALVES - 1)
+            rectified = held.tile([P, CHUNK], F32, name=f"rectified{chunk}")
+            nc.scalar.activation(rectified[:], effect[:], RELU, bias=b3_sb[:])
+            result = held.tile([P, CHUNK], F32, name=f"result{chunk}")
+            nc.vector.tensor_tensor(result[:], rectified[:], recv_sb[:, cols], ADD)
+            nc.sync.dma_start(out[:, cols], result[:])

@@ -1,4 +1,5 @@
 import concourse.mybir as mybir
+from concourse.masks import make_identity
 
 BF16, F32, U16 = mybir.dt.bfloat16, mybir.dt.float32, mybir.dt.uint16
 RELU = mybir.ActivationFunctionType.Relu
@@ -22,23 +23,20 @@ def tile_physics_kernel(tc, table, w, recv, w_recv, b1, w3, b3, offs, out):
         offsets = held.tile([P, N // 16], U16, name="offsets")
         nc.sync.dma_start(offsets[:], offs)
         table_sb = held.tile([P, S], BF16, name="table_sb")
-        nc.sync.dma_start(table_sb[:], table)
+        nc.scalar.dma_start(table_sb[:], table)
         w_sb = held.tile([P, M], BF16, name="w_sb")
-        nc.scalar.dma_start(w_sb[:], w)
+        nc.sync.dma_start(w_sb[:], w)
         w_recv_sb = held.tile([P, M], BF16, name="w_recv_sb")
         nc.scalar.dma_start(w_recv_sb[:], w_recv)
         recv_sb = held.tile([P, N], BF16, name="recv_sb")
         nc.sync.dma_start(recv_sb[:], recv)
-        b1_sb = []
-        w3_sb = []
-        for half in range(HALVES):
-            rows = slice(half * P, (half + 1) * P)
-            b1_sb.append(held.tile([P, 1], F32, name=f"b1_sb{half}"))
-            nc.gpsimd.dma_start(b1_sb[half][:], b1[rows, :])
-            w3_sb.append(held.tile([P, P], BF16, name=f"w3_sb{half}"))
-            nc.sync.dma_start(w3_sb[half][:], w3[rows, :])
+        w3_sb = held.tile([P, HALVES, P], BF16, name="w3_sb")
+        nc.scalar.dma_start(w3_sb[:], w3.rearrange("(half p) d -> p half d", p=P))
+        b1_sb = held.tile([P, HALVES], F32, name="b1_sb")
+        with nc.allow_non_contiguous_dma(reason="one float32 of b1 for each partition and half"):
+            nc.sync.dma_start(b1_sb[:], b1.rearrange("(half p) one -> p (half one)", p=P))
         b3_sb = held.tile([P, 1], F32, name="b3_sb")
-        nc.gpsimd.dma_start(b3_sb[:], b3)
+        nc.sync.dma_start(b3_sb[:], b3)
 
         zeros = held.tile([P, P], BF16, name="zeros")
         nc.vector.memset(zeros[:], 0.0)
@@ -47,6 +45,9 @@ def tile_physics_kernel(tc, table, w, recv, w_recv, b1, w3, b3, offs, out):
             nc.tensor.matmul(unread[:], zeros[:], zeros[:].unsqueeze(1).to_broadcast([P, N // P, P]), start=True, stop=True)
         unread_relu = held.tile([P, 1], BF16, name="unread_relu")
         nc.scalar.activation(unread_relu[:], zeros[:, 0:1], RELU)
+
+        identity = held.tile([P, P], BF16, name="identity")
+        make_identity(nc, identity[:])
 
         hidden = {}
         for chunk in range(CHUNKS):
@@ -59,17 +60,16 @@ def tile_physics_kernel(tc, table, w, recv, w_recv, b1, w3, b3, offs, out):
                 nc.tensor.matmul(pre[:], w_recv_sb[:, units], recv_sb[:, cols], start=False, stop=True)
                 hidden[chunk, half] = held.tile([P, CHUNK], BF16, name=f"hidden{chunk}_{half}")
                 if half == 0:
-                    nc.scalar.activation(hidden[chunk, half][:], pre[:], RELU, bias=b1_sb[half][:])
+                    nc.scalar.activation(hidden[chunk, half][:], pre[:], RELU, bias=b1_sb[:, half : half + 1])
                 else:
-                    nc.vector.tensor_scalar(hidden[chunk, half][:], pre[:], b1_sb[half][:], 0.0, ADD, MAX)
+                    nc.vector.tensor_scalar(hidden[chunk, half][:], pre[:], b1_sb[:, half : half + 1], 0.0, ADD, MAX)
 
         for chunk in range(CHUNKS):
             cols = slice(chunk * CHUNK, (chunk + 1) * CHUNK)
             effect = psum.tile([P, CHUNK], F32, name=f"effect{chunk}")
+            nc.tensor.matmul(effect[:], identity[:], recv_sb[:, cols], start=True, stop=False)
             for half in range(HALVES):
-                nc.tensor.matmul(effect[:], w3_sb[half][:], hidden[chunk, half][:], start=half == 0, stop=half == HALVES - 1)
-            rectified = held.tile([P, CHUNK], F32, name=f"rectified{chunk}")
-            nc.scalar.activation(rectified[:], effect[:], RELU, bias=b3_sb[:])
+                nc.tensor.matmul(effect[:], w3_sb[:, half, :], hidden[chunk, half][:], start=False, stop=half == HALVES - 1)
             result = held.tile([P, CHUNK], F32, name=f"result{chunk}")
-            nc.vector.tensor_tensor(result[:], rectified[:], recv_sb[:, cols], ADD)
+            nc.vector.scalar_tensor_tensor(result[:], effect[:], b3_sb[:], recv_sb[:, cols], ADD, MAX)
             nc.sync.dma_start(out[:, cols], result[:])

@@ -12,7 +12,6 @@ M = 256
 HALVES = M // P
 CHUNK = 256
 CHUNKS = N // CHUNK
-WARM_UP_MATMULS = 4
 
 FLOPS = 2 * N * (P * M + P * M + M * P)
 
@@ -38,11 +37,8 @@ def tile_physics_kernel(tc, table, w, recv, w_recv, b1, w3, b3, offs, out):
         b3_sb = held.tile([P, 1], F32, name="b3_sb")
         nc.sync.dma_start(b3_sb[:], b3)
 
-        zeros = held.tile([P, P], BF16, name="zeros")
+        zeros = held.tile([P, 1], BF16, name="zeros")
         nc.vector.memset(zeros[:], 0.0)
-        unread = psum.tile([P, N // P, P], F32, name="unread")
-        for repeat in range(WARM_UP_MATMULS):
-            nc.tensor.matmul(unread[:], zeros[:], zeros[:].unsqueeze(1).to_broadcast([P, N // P, P]), start=True, stop=True)
         unread_relu = held.tile([P, 1], BF16, name="unread_relu")
         nc.scalar.activation(unread_relu[:], zeros[:, 0:1], RELU)
 

@@ -12,13 +12,19 @@ M = 256
 HALVES = M // P
 CHUNK = 256
 CHUNKS = N // CHUNK
+WARM_UP_MATMULS = 2
 
 FLOPS = 2 * N * (P * M + P * M + M * P)
 
 
 def tile_physics_kernel(tc, table, w, recv, w_recv, b1, w3, b3, offs, out):
     nc = tc.nc
-    with tc.tile_pool(name="held", bufs=1) as held, tc.psum_pool(name="psum", bufs=1) as psum:
+    with (
+        tc.tile_pool(name="held", bufs=1) as held,
+        tc.psum_pool(name="warm", bufs=1) as warm,
+        tc.psum_pool(name="layer1", bufs=4) as layer1,
+        tc.psum_pool(name="layer2", bufs=2) as layer2,
+    ):
         offsets = held.tile([P, N // 16], U16, name="offsets")
         nc.sync.dma_start(offsets[:], offs)
         table_sb = held.tile([P, S], BF16, name="table_sb")
@@ -37,8 +43,11 @@ def tile_physics_kernel(tc, table, w, recv, w_recv, b1, w3, b3, offs, out):
         b3_sb = held.tile([P, 1], F32, name="b3_sb")
         nc.sync.dma_start(b3_sb[:], b3)
 
-        zeros = held.tile([P, 1], BF16, name="zeros")
+        zeros = held.tile([P, P], BF16, name="zeros")
         nc.vector.memset(zeros[:], 0.0)
+        unread = warm.tile([P, N // P, P], F32, name="unread")
+        for repeat in range(WARM_UP_MATMULS):
+            nc.tensor.matmul(unread[:], zeros[:], zeros[:].unsqueeze(1).to_broadcast([P, N // P, P]), start=True, stop=True)
         unread_relu = held.tile([P, 1], BF16, name="unread_relu")
         nc.scalar.activation(unread_relu[:], zeros[:, 0:1], RELU)
 
@@ -51,7 +60,7 @@ def tile_physics_kernel(tc, table, w, recv, w_recv, b1, w3, b3, offs, out):
             senders = table_sb[:].indirect(offsets[:, chunk * CHUNK // 16 : (chunk + 1) * CHUNK // 16])
             for half in range(HALVES):
                 units = slice(half * P, (half + 1) * P)
-                pre = psum.tile([P, CHUNK], F32, name=f"pre{chunk}_{half}")
+                pre = layer1.tile([P, CHUNK], F32, name="pre")
                 nc.tensor.matmul(pre[:], w_sb[:, units], senders, start=True, stop=False)
                 nc.tensor.matmul(pre[:], w_recv_sb[:, units], recv_sb[:, cols], start=False, stop=True)
                 hidden[chunk, half] = held.tile([P, CHUNK], BF16, name=f"hidden{chunk}_{half}")
@@ -62,7 +71,7 @@ def tile_physics_kernel(tc, table, w, recv, w_recv, b1, w3, b3, offs, out):
 
         for chunk in range(CHUNKS):
             cols = slice(chunk * CHUNK, (chunk + 1) * CHUNK)
-            effect = psum.tile([P, CHUNK], F32, name=f"effect{chunk}")
+            effect = layer2.tile([P, CHUNK], F32, name="effect")
             nc.tensor.matmul(effect[:], identity[:], recv_sb[:, cols], start=True, stop=False)
             for half in range(HALVES):
                 nc.tensor.matmul(effect[:], w3_sb[:, half, :], hidden[chunk, half][:], start=False, stop=half == HALVES - 1)

@@ -12,7 +12,7 @@ M = 256
 HALVES = M // P
 CHUNK = 256
 CHUNKS = N // CHUNK
-WARM_UP_MATMULS = 2
+WARM_UP_MATMULS = 3
 
 FLOPS = 2 * N * (P * M + P * M + M * P)
 

@@ -22,25 +22,27 @@ def tile_physics_kernel(tc, table, w, recv, w_recv, b1, w3, b3, offs, out):
     with (
         tc.tile_pool(name="held", bufs=1) as held,
         tc.psum_pool(name="warm", bufs=1) as warm,
-        tc.psum_pool(name="layer1", bufs=4) as layer1,
-        tc.psum_pool(name="layer2", bufs=2) as layer2,
+        tc.psum_pool(name="layer1", bufs=1) as layer1,
+        tc.psum_pool(name="layer2", bufs=1) as layer2,
     ):
-        offsets = held.tile([P, N // 16], U16, name="offsets")
-        nc.sync.dma_start(offsets[:], offs)
-        table_sb = held.tile([P, S], BF16, name="table_sb")
-        nc.scalar.dma_start(table_sb[:], table)
-        w_sb = held.tile([P, M], BF16, name="w_sb")
-        nc.sync.dma_start(w_sb[:], w)
-        w_recv_sb = held.tile([P, M], BF16, name="w_recv_sb")
-        nc.scalar.dma_start(w_recv_sb[:], w_recv)
         recv_sb = held.tile([P, N], BF16, name="recv_sb")
-        nc.sync.dma_start(recv_sb[:], recv)
-        w3_sb = held.tile([P, HALVES, P], BF16, name="w3_sb")
-        nc.scalar.dma_start(w3_sb[:], w3.rearrange("(half p) d -> p half d", p=P))
+        w_recv_sb = held.tile([P, M], BF16, name="w_recv_sb")
+        offsets = held.tile([P, N // 16], U16, name="offsets")
+        w_sb = held.tile([P, M], BF16, name="w_sb")
+        table_sb = held.tile([P, S], BF16, name="table_sb")
         b1_sb = held.tile([P, HALVES], F32, name="b1_sb")
+        w3_sb = held.tile([P, HALVES, P], BF16, name="w3_sb")
+        b3_sb = held.tile([P, 1], F32, name="b3_sb")
+        nc.scalar.dma_start(w_recv_sb[:], w_recv)
+        for chunk in range(CHUNKS):
+            cols = slice(chunk * CHUNK, (chunk + 1) * CHUNK)
+            nc.sync.dma_start(recv_sb[:, cols], recv[:, cols])
+        nc.scalar.dma_start(table_sb[:], table)
+        nc.sync.dma_start(offsets[:], offs)
+        nc.sync.dma_start(w_sb[:], w)
         with nc.allow_non_contiguous_dma(reason="one float32 of b1 for each partition and half"):
             nc.sync.dma_start(b1_sb[:], b1.rearrange("(half p) one -> p (half one)", p=P))
-        b3_sb = held.tile([P, 1], F32, name="b3_sb")
+        nc.scalar.dma_start(w3_sb[:], w3.rearrange("(half p) d -> p half d", p=P))
         nc.sync.dma_start(b3_sb[:], b3)
 
         zeros = held.tile([P, P], BF16, name="zeros")
@@ -54,27 +56,32 @@ def tile_physics_kernel(tc, table, w, recv, w_recv, b1, w3, b3, offs, out):
         identity = held.tile([P, P], BF16, name="identity")
         make_identity(nc, identity[:])
 
-        hidden = {}
+        pre, effect = {}, {}
         for chunk in range(CHUNKS):
             cols = slice(chunk * CHUNK, (chunk + 1) * CHUNK)
+            effect[chunk] = layer2.tile([P, CHUNK], F32, name=f"effect{chunk}")
+            nc.tensor.matmul(effect[chunk][:], identity[:], recv_sb[:, cols], start=True, stop=False)
+            for half in range(HALVES):
+                units = slice(half * P, (half + 1) * P)
+                pre[chunk, half] = layer1.tile([P, CHUNK], F32, name=f"pre{chunk}_{half}")
+                nc.tensor.matmul(pre[chunk, half][:], w_recv_sb[:, units], recv_sb[:, cols], start=True, stop=False)
+
+        hidden = {}
+        for chunk in range(CHUNKS):
             senders = table_sb[:].indirect(offsets[:, chunk * CHUNK // 16 : (chunk + 1) * CHUNK // 16])
             for half in range(HALVES):
                 units = slice(half * P, (half + 1) * P)
-                pre = layer1.tile([P, CHUNK], F32, name="pre")
-                nc.tensor.matmul(pre[:], w_sb[:, units], senders, start=True, stop=False)
-                nc.tensor.matmul(pre[:], w_recv_sb[:, units], recv_sb[:, cols], start=False, stop=True)
+                nc.tensor.matmul(pre[chunk, half][:], w_sb[:, units], senders, start=False, stop=True)
                 hidden[chunk, half] = held.tile([P, CHUNK], BF16, name=f"hidden{chunk}_{half}")
                 if half == 0:
-                    nc.scalar.activation(hidden[chunk, half][:], pre[:], RELU, bias=b1_sb[:, half : half + 1])
+                    nc.scalar.activation(hidden[chunk, half][:], pre[chunk, half][:], RELU, bias=b1_sb[:, half : half + 1])
                 else:
-                    nc.vector.tensor_scalar(hidden[chunk, half][:], pre[:], b1_sb[:, half : half + 1], 0.0, ADD, MAX)
+                    nc.vector.tensor_scalar(hidden[chunk, half][:], pre[chunk, half][:], b1_sb[:, half : half + 1], 0.0, ADD, MAX)
 
         for chunk in range(CHUNKS):
             cols = slice(chunk * CHUNK, (chunk + 1) * CHUNK)
-            effect = layer2.tile([P, CHUNK], F32, name="effect")
-            nc.tensor.matmul(effect[:], identity[:], recv_sb[:, cols], start=True, stop=False)
             for half in range(HALVES):
-                nc.tensor.matmul(effect[:], w3_sb[:, half, :], hidden[chunk, half][:], start=False, stop=half == HALVES - 1)
+                nc.tensor.matmul(effect[chunk][:], w3_sb[:, half, :], hidden[chunk, half][:], start=False, stop=half == HALVES - 1)
             result = held.tile([P, CHUNK], F32, name=f"result{chunk}")
-            nc.vector.scalar_tensor_tensor(result[:], effect[:], b3_sb[:], recv_sb[:, cols], ADD, MAX)
+            nc.vector.scalar_tensor_tensor(result[:], effect[chunk][:], b3_sb[:], recv_sb[:, cols], ADD, MAX)
             nc.sync.dma_start(out[:, cols], result[:])

@@ -12,7 +12,6 @@ M = 256
 HALVES = M // P
 CHUNK = 256
 CHUNKS = N // CHUNK
-WARM_UP_MATMULS = 3
 
 FLOPS = 2 * N * (P * M + P * M + M * P)
 
@@ -21,7 +20,6 @@ def tile_physics_kernel(tc, table, w, recv, w_recv, b1, w3, b3, offs, out):
     nc = tc.nc
     with (
         tc.tile_pool(name="held", bufs=1) as held,
-        tc.psum_pool(name="warm", bufs=1) as warm,
         tc.psum_pool(name="layer1", bufs=1) as layer1,
         tc.psum_pool(name="layer2", bufs=1) as layer2,
     ):
@@ -45,13 +43,10 @@ def tile_physics_kernel(tc, table, w, recv, w_recv, b1, w3, b3, offs, out):
         nc.scalar.dma_start(w3_sb[:], w3.rearrange("(half p) d -> p half d", p=P))
         nc.sync.dma_start(b3_sb[:], b3)
 
-        zeros = held.tile([P, P], BF16, name="zeros")
-        nc.vector.memset(zeros[:], 0.0)
-        unread = warm.tile([P, N // P, P], F32, name="unread")
-        for repeat in range(WARM_UP_MATMULS):
-            nc.tensor.matmul(unread[:], zeros[:], zeros[:].unsqueeze(1).to_broadcast([P, N // P, P]), start=True, stop=True)
+        zeros = held.tile([P, 1], BF16, name="zeros")
+        nc.gpsimd.memset(zeros[:], 0.0)
         unread_relu = held.tile([P, 1], BF16, name="unread_relu")
-        nc.scalar.activation(unread_relu[:], zeros[:, 0:1], RELU)
+        nc.scalar.activation(unread_relu[:], zeros[:], RELU)
 
         identity = held.tile([P, P], BF16, name="identity")
         make_identity(nc, identity[:])

@@ -31,16 +31,15 @@ def tile_physics_kernel(tc, table, w, recv, w_recv, b1, w3, b3, offs, out):
         b1_sb = held.tile([P, HALVES], F32, name="b1_sb")
         w3_sb = held.tile([P, HALVES, P], BF16, name="w3_sb")
         b3_sb = held.tile([P, 1], F32, name="b3_sb")
+        nc.sync.dma_start(recv_sb[:, 0:CHUNK], recv[:, 0:CHUNK])
         nc.scalar.dma_start(w_recv_sb[:], w_recv)
-        for chunk in range(CHUNKS):
-            cols = slice(chunk * CHUNK, (chunk + 1) * CHUNK)
-            nc.sync.dma_start(recv_sb[:, cols], recv[:, cols])
-        nc.scalar.dma_start(table_sb[:], table)
         nc.sync.dma_start(offsets[:], offs)
-        nc.sync.dma_start(w_sb[:], w)
+        nc.scalar.dma_start(recv_sb[:, CHUNK:N], recv[:, CHUNK:N])
+        nc.sync.dma_start(table_sb[:], table)
+        nc.scalar.dma_start(w_sb[:], w)
         with nc.allow_non_contiguous_dma(reason="one float32 of b1 for each partition and half"):
             nc.sync.dma_start(b1_sb[:], b1.rearrange("(half p) one -> p (half one)", p=P))
-        nc.scalar.dma_start(w3_sb[:], w3.rearrange("(half p) d -> p half d", p=P))
+        nc.sync.dma_start(w3_sb[:], w3.rearrange("(half p) d -> p half d", p=P))
         nc.sync.dma_start(b3_sb[:], b3)
 
         zeros = held.tile([P, 1], BF16, name="zeros")

@@ -2,7 +2,6 @@ import concourse.mybir as mybir
 from concourse.masks import make_identity
 
 BF16, F32, U16 = mybir.dt.bfloat16, mybir.dt.float32, mybir.dt.uint16
-RELU = mybir.ActivationFunctionType.Relu
 ADD, MAX = mybir.AluOpType.add, mybir.AluOpType.max
 
 P = 128
@@ -42,11 +41,6 @@ def tile_physics_kernel(tc, table, w, recv, w_recv, b1, w3, b3, offs, out):
         nc.sync.dma_start(w3_sb[:], w3.rearrange("(half p) d -> p half d", p=P))
         nc.sync.dma_start(b3_sb[:], b3)
 
-        zeros = held.tile([P, 1], BF16, name="zeros")
-        nc.gpsimd.memset(zeros[:], 0.0)
-        unread_relu = held.tile([P, 1], BF16, name="unread_relu")
-        nc.scalar.activation(unread_relu[:], zeros[:], RELU)
-
         identity = held.tile([P, P], BF16, name="identity")
         make_identity(nc, identity[:])
 
@@ -67,10 +61,7 @@ def tile_physics_kernel(tc, table, w, recv, w_recv, b1, w3, b3, offs, out):
                 units = slice(half * P, (half + 1) * P)
                 nc.tensor.matmul(pre[chunk, half][:], w_sb[:, units], senders, start=False, stop=True)
                 hidden[chunk, half] = held.tile([P, CHUNK], BF16, name=f"hidden{chunk}_{half}")
-                if half == 0:
-                    nc.scalar.activation(hidden[chunk, half][:], pre[chunk, half][:], RELU, bias=b1_sb[:, half : half + 1])
-                else:
-                    nc.vector.tensor_scalar(hidden[chunk, half][:], pre[chunk, half][:], b1_sb[:, half : half + 1], 0.0, ADD, MAX)
+                nc.vector.tensor_scalar(hidden[chunk, half][:], pre[chunk, half][:], b1_sb[:, half : half + 1], 0.0, ADD, MAX)
 
         for chunk in range(CHUNKS):
             cols = slice(chunk * CHUNK, (chunk + 1) * CHUNK)

@@ -11,6 +11,7 @@ M = 256
 HALVES = M // P
 CHUNK = 256
 CHUNKS = N // CHUNK
+WARM_UP_MATMULS = 3
 
 FLOPS = 2 * N * (P * M + P * M + M * P)
 
@@ -19,6 +20,7 @@ def tile_physics_kernel(tc, table, w, recv, w_recv, b1, w3, b3, offs, out):
     nc = tc.nc
     with (
         tc.tile_pool(name="held", bufs=1) as held,
+        tc.psum_pool(name="warm", bufs=1) as warm,
         tc.psum_pool(name="layer1", bufs=1) as layer1,
         tc.psum_pool(name="layer2", bufs=1) as layer2,
     ):
@@ -40,6 +42,12 @@ def tile_physics_kernel(tc, table, w, recv, w_recv, b1, w3, b3, offs, out):
             nc.sync.dma_start(b1_sb[:], b1.rearrange("(half p) one -> p (half one)", p=P))
         nc.sync.dma_start(w3_sb[:], w3.rearrange("(half p) d -> p half d", p=P))
         nc.sync.dma_start(b3_sb[:], b3)
+
+        zeros = held.tile([P, P], BF16, name="zeros")
+        nc.vector.memset(zeros[:], 0.0)
+        unread = warm.tile([P, N // P, P], F32, name="unread")
+        for repeat in range(WARM_UP_MATMULS):
+            nc.tensor.matmul(unread[:], zeros[:], zeros[:].unsqueeze(1).to_broadcast([P, N // P, P]), start=True, stop=True)
 
         identity = held.tile([P, P], BF16, name="identity")
         make_identity(nc, identity[:])

@@ -38,9 +38,9 @@ def tile_physics_kernel(tc, table, w, recv, w_recv, b1, w3, b3, offs, out):
         nc.scalar.dma_start(recv_sb[:, CHUNK:N], recv[:, CHUNK:N])
         nc.sync.dma_start(table_sb[:], table)
         nc.scalar.dma_start(w_sb[:], w)
-        with nc.allow_non_contiguous_dma(reason="one float32 of b1 for each partition and half"):
-            nc.sync.dma_start(b1_sb[:], b1.rearrange("(half p) one -> p (half one)", p=P))
-        nc.sync.dma_start(w3_sb[:], w3.rearrange("(half p) d -> p half d", p=P))
+        with nc.allow_non_contiguous_dma(reason="one float32 of b1 for each partition"):
+            nc.sync.dma_start(b1_sb[:], b1.rearrange("(p half) one -> p (half one)", half=HALVES))
+        nc.sync.dma_start(w3_sb[:], w3.rearrange("(p half) d -> p half d", half=HALVES))
         nc.sync.dma_start(b3_sb[:], b3)
 
         zeros = held.tile([P, P], BF16, name="zeros")
@@ -58,7 +58,7 @@ def tile_physics_kernel(tc, table, w, recv, w_recv, b1, w3, b3, offs, out):
             effect[chunk] = layer2.tile([P, CHUNK], F32, name=f"effect{chunk}")
             nc.tensor.matmul(effect[chunk][:], identity[:], recv_sb[:, cols], start=True, stop=False)
             for half in range(HALVES):
-                units = slice(half * P, (half + 1) * P)
+                units = slice(half, M, HALVES)
                 pre[chunk, half] = layer1.tile([P, CHUNK], F32, name=f"pre{chunk}_{half}")
                 nc.tensor.matmul(pre[chunk, half][:], w_recv_sb[:, units], recv_sb[:, cols], start=True, stop=False)
 
@@ -66,7 +66,7 @@ def tile_physics_kernel(tc, table, w, recv, w_recv, b1, w3, b3, offs, out):
         for chunk in range(CHUNKS):
             senders = table_sb[:].indirect(offsets[:, chunk * CHUNK // 16 : (chunk + 1) * CHUNK // 16])
             for half in range(HALVES):
-                units = slice(half * P, (half + 1) * P)
+                units = slice(half, M, HALVES)
                 nc.tensor.matmul(pre[chunk, half][:], w_sb[:, units], senders, start=False, stop=True)
                 hidden[chunk, half] = held.tile([P, CHUNK], BF16, name=f"hidden{chunk}_{half}")
                 nc.vector.tensor_scalar(hidden[chunk, half][:], pre[chunk, half][:], b1_sb[:, half : half + 1], 0.0, ADD, MAX)

@@ -11,6 +11,7 @@ M = 256
 HALVES = M // P
 CHUNK = 256
 CHUNKS = N // CHUNK
+LAST = (CHUNKS - 1, HALVES - 1)
 WARM_UP_MATMULS = 3
 
 FLOPS = 2 * N * (P * M + P * M + M * P)
@@ -60,14 +61,19 @@ def tile_physics_kernel(tc, table, w, recv, w_recv, b1, w3, b3, offs, out):
             for half in range(HALVES):
                 units = slice(half, M, HALVES)
                 pre[chunk, half] = layer1.tile([P, CHUNK], F32, name=f"pre{chunk}_{half}")
-                nc.tensor.matmul(pre[chunk, half][:], w_recv_sb[:, units], recv_sb[:, cols], start=True, stop=False)
+                if (chunk, half) != LAST:
+                    nc.tensor.matmul(pre[chunk, half][:], w_recv_sb[:, units], recv_sb[:, cols], start=True, stop=False)
 
         hidden = {}
         for chunk in range(CHUNKS):
             senders = table_sb[:].indirect(offsets[:, chunk * CHUNK // 16 : (chunk + 1) * CHUNK // 16])
             for half in range(HALVES):
                 units = slice(half, M, HALVES)
-                nc.tensor.matmul(pre[chunk, half][:], w_sb[:, units], senders, start=False, stop=True)
+                is_last = (chunk, half) == LAST
+                nc.tensor.matmul(pre[chunk, half][:], w_sb[:, units], senders, start=is_last, stop=not is_last)
+                if is_last:
+                    cols = slice(chunk * CHUNK, (chunk + 1) * CHUNK)
+                    nc.tensor.matmul(pre[chunk, half][:], w_recv_sb[:, units], recv_sb[:, cols], start=False, stop=True)
                 hidden[chunk, half] = held.tile([P, CHUNK], BF16, name=f"hidden{chunk}_{half}")
                 nc.vector.tensor_scalar(hidden[chunk, half][:], pre[chunk, half][:], b1_sb[:, half : half + 1], 0.0, ADD, MAX)
 

@@ -11,6 +11,7 @@ M = 256
 HALVES = M // P
 CHUNK = 256
 CHUNKS = N // CHUNK
+PIECES = [(0, 0, 256), (1, 256, 384), (1, 384, 512)]
 LAST = (CHUNKS - 1, HALVES - 1)
 WARM_UP_MATMULS = 3
 
@@ -53,11 +54,9 @@ def tile_physics_kernel(tc, table, w, recv, w_recv, b1, w3, b3, offs, out):
         identity = held.tile([P, P], BF16, name="identity")
         make_identity(nc, identity[:])
 
-        pre, effect = {}, {}
+        pre = {}
         for chunk in range(CHUNKS):
             cols = slice(chunk * CHUNK, (chunk + 1) * CHUNK)
-            effect[chunk] = layer2.tile([P, CHUNK], F32, name=f"effect{chunk}")
-            nc.tensor.matmul(effect[chunk][:], identity[:], recv_sb[:, cols], start=True, stop=False)
             for half in range(HALVES):
                 units = slice(half, M, HALVES)
                 pre[chunk, half] = layer1.tile([P, CHUNK], F32, name=f"pre{chunk}_{half}")
@@ -77,10 +76,17 @@ def tile_physics_kernel(tc, table, w, recv, w_recv, b1, w3, b3, offs, out):
                 hidden[chunk, half] = held.tile([P, CHUNK], BF16, name=f"hidden{chunk}_{half}")
                 nc.vector.tensor_scalar(hidden[chunk, half][:], pre[chunk, half][:], b1_sb[:, half : half + 1], 0.0, ADD, MAX)
 
-        for chunk in range(CHUNKS):
-            cols = slice(chunk * CHUNK, (chunk + 1) * CHUNK)
+        for pieces in (PIECES[:1], PIECES[1:]):
+            effect = {}
+            for chunk, first, end in pieces:
+                effect[first] = layer2.tile([P, end - first], F32, name=f"effect{first}")
+                nc.tensor.matmul(effect[first][:], identity[:], recv_sb[:, first:end], start=True, stop=False)
             for half in range(HALVES):
-                nc.tensor.matmul(effect[chunk][:], w3_sb[:, half, :], hidden[chunk, half][:], start=False, stop=half == HALVES - 1)
-            result = held.tile([P, CHUNK], F32, name=f"result{chunk}")
-            nc.vector.scalar_tensor_tensor(result[:], effect[chunk][:], b3_sb[:], recv_sb[:, cols], ADD, MAX)
-            nc.sync.dma_start(out[:, cols], result[:])
+                for chunk, first, end in pieces:
+                    part = slice(first - chunk * CHUNK, end - chunk * CHUNK)
+                    nc.tensor.matmul(effect[first][:], w3_sb[:, half, :], hidden[chunk, half][:, part], start=False, stop=half == HALVES - 1)
+            for chunk, first, end in pieces:
+                result = held.tile([P, end - first], F32, name=f"result{first}")
+                nc.vector.scalar_tensor_tensor(result[:], effect[first][:], b3_sb[:], recv_sb[:, first:end], ADD, MAX)
+                queue = nc.scalar if first == CHUNK else nc.sync
+                queue.dma_start(out[:, first:end], result[:])

import concourse.mybir as mybir
from concourse.masks import make_identity

BF16, F32, U16 = mybir.dt.bfloat16, mybir.dt.float32, mybir.dt.uint16
ADD, MAX = mybir.AluOpType.add, mybir.AluOpType.max

P = 128
S = 512
N = 512
M = 256
HALVES = M // P
CHUNK = 256
CHUNKS = N // CHUNK
PIECES = [(0, 0, 256), (1, 256, 384), (1, 384, 512)]
LAST = (CHUNKS - 1, HALVES - 1)
WARM_UP_MATMULS = 3

FLOPS = 2 * N * (P * M + P * M + M * P)


def tile_physics_kernel(tc, table, w, recv, w_recv, b1, w3, b3, offs, out):
    nc = tc.nc
    with (
        tc.tile_pool(name="held", bufs=1) as held,
        tc.psum_pool(name="warm", bufs=1) as warm,
        tc.psum_pool(name="layer1", bufs=1) as layer1,
        tc.psum_pool(name="layer2", bufs=1) as layer2,
    ):
        recv_sb = held.tile([P, N], BF16, name="recv_sb")
        w_recv_sb = held.tile([P, M], BF16, name="w_recv_sb")
        offsets = held.tile([P, N // 16], U16, name="offsets")
        w_sb = held.tile([P, M], BF16, name="w_sb")
        table_sb = held.tile([P, S], BF16, name="table_sb")
        b1_sb = held.tile([P, HALVES], F32, name="b1_sb")
        w3_sb = held.tile([P, HALVES, P], BF16, name="w3_sb")
        b3_sb = held.tile([P, 1], F32, name="b3_sb")
        nc.sync.dma_start(recv_sb[:, 0:CHUNK], recv[:, 0:CHUNK])
        nc.scalar.dma_start(w_recv_sb[:], w_recv)
        nc.sync.dma_start(offsets[:], offs)
        nc.scalar.dma_start(recv_sb[:, CHUNK:N], recv[:, CHUNK:N])
        nc.sync.dma_start(table_sb[:], table)
        nc.scalar.dma_start(w_sb[:], w)
        with nc.allow_non_contiguous_dma(reason="one float32 of b1 for each partition"):
            nc.sync.dma_start(b1_sb[:], b1.rearrange("(p half) one -> p (half one)", half=HALVES))
        nc.sync.dma_start(w3_sb[:], w3.rearrange("(p half) d -> p half d", half=HALVES))
        nc.sync.dma_start(b3_sb[:], b3)

        zeros = held.tile([P, P], BF16, name="zeros")
        nc.vector.memset(zeros[:], 0.0)
        unread = warm.tile([P, N // P, P], F32, name="unread")
        for repeat in range(WARM_UP_MATMULS):
            nc.tensor.matmul(unread[:], zeros[:], zeros[:].unsqueeze(1).to_broadcast([P, N // P, P]), start=True, stop=True)

        identity = held.tile([P, P], BF16, name="identity")
        make_identity(nc, identity[:])

        pre = {}
        for chunk in range(CHUNKS):
            cols = slice(chunk * CHUNK, (chunk + 1) * CHUNK)
            for half in range(HALVES):
                units = slice(half, M, HALVES)
                pre[chunk, half] = layer1.tile([P, CHUNK], F32, name=f"pre{chunk}_{half}")
                if (chunk, half) != LAST:
                    nc.tensor.matmul(pre[chunk, half][:], w_recv_sb[:, units], recv_sb[:, cols], start=True, stop=False)

        hidden = {}
        for chunk in range(CHUNKS):
            senders = table_sb[:].indirect(offsets[:, chunk * CHUNK // 16 : (chunk + 1) * CHUNK // 16])
            for half in range(HALVES):
                units = slice(half, M, HALVES)
                is_last = (chunk, half) == LAST
                nc.tensor.matmul(pre[chunk, half][:], w_sb[:, units], senders, start=is_last, stop=not is_last)
                if is_last:
                    cols = slice(chunk * CHUNK, (chunk + 1) * CHUNK)
                    nc.tensor.matmul(pre[chunk, half][:], w_recv_sb[:, units], recv_sb[:, cols], start=False, stop=True)
                hidden[chunk, half] = held.tile([P, CHUNK], BF16, name=f"hidden{chunk}_{half}")
                nc.vector.tensor_scalar(hidden[chunk, half][:], pre[chunk, half][:], b1_sb[:, half : half + 1], 0.0, ADD, MAX)

        for pieces in (PIECES[:1], PIECES[1:]):
            effect = {}
            for chunk, first, end in pieces:
                effect[first] = layer2.tile([P, end - first], F32, name=f"effect{first}")
                nc.tensor.matmul(effect[first][:], identity[:], recv_sb[:, first:end], start=True, stop=False)
            for half in range(HALVES):
                for chunk, first, end in pieces:
                    part = slice(first - chunk * CHUNK, end - chunk * CHUNK)
                    nc.tensor.matmul(effect[first][:], w3_sb[:, half, :], hidden[chunk, half][:, part], start=False, stop=half == HALVES - 1)
            for chunk, first, end in pieces:
                result = held.tile([P, end - first], F32, name=f"result{first}")
                nc.vector.scalar_tensor_tensor(result[:], effect[first][:], b3_sb[:], recv_sb[:, first:end], ADD, MAX)
                queue = nc.scalar if first == CHUNK else nc.sync
                queue.dma_start(out[:, first:end], result[:])
